import numpy as np
import ml_dtypes


def mxq(x, axis, fmt="e4m3"):
    dtype, down = {"e4m3": (ml_dtypes.float8_e4m3fn, 7), "e5m2": (ml_dtypes.float8_e5m2, 14)}[fmt]
    v = np.moveaxis(np.asarray(x, np.float32).astype(ml_dtypes.bfloat16).astype(np.float64), axis, -1)
    blocks = v.reshape(v.shape[:-1] + (-1, 32))
    amax = np.abs(blocks).max(-1, keepdims=True)
    byte = np.maximum(np.where(amax > 0, np.frexp(amax)[1] - 1 + 127, 0) - down, 1)
    scale = np.exp2(byte - 127.0)
    codes = (blocks / scale).astype(np.float32).astype(dtype).astype(np.float64)
    return np.moveaxis((codes * scale).reshape(v.shape), -1, axis)


WIDE = False


def mx_kscale(k):
    if not WIDE:
        return np.ones(k)
    levels = np.array([10, -10, 5, -5, 0])
    if k % 512:
        return np.exp2(np.random.permutation(np.resize(levels, k // 32))).repeat(32)
    a = np.empty((k // 512, 16))
    for p in range(k // 512):
        a[p, :8] = np.random.permutation(np.resize(levels, 8))
        for g in range(8):
            far = levels[np.abs(levels - a[p, g]) >= 10]
            a[p, g + 8] = far[np.random.randint(len(far))]
    return np.exp2(a.ravel()).repeat(32)


BF16 = ml_dtypes.bfloat16


def bf(x):
    return np.asarray(x, np.float32).astype(BF16)


def f64(x):
    return np.asarray(x).astype(np.float64)


B, N_EP, S, D, IN_DIM, L, K = 6, 3, 512, 256, 255, 512, 10


def setup_inputs():
    s, t = mx_kscale(S), mx_kscale(L)
    r = np.random.standard_normal
    g = r((B, S, S)) * 1.56
    a = np.exp(g - g.max(-1, keepdims=True))
    a = a / a.sum(-1, keepdims=True)
    return {"attn1": bf(a * s), "v1": bf(r((B, S, L)) * 4.0 / s[:, None] * t),
            "Wq2": bf(r((L, L)) * 4.0 / np.sqrt(L) / t[:, None]), "bq2": bf(r(L) * 0.2),
            "Wk2": bf(r((L, L)) * 4.0 / np.sqrt(L) / t[:, None]), "bk2": bf(r(L) * 0.2),
            "Wv2": bf(r((L, L)) * 3.2 / np.sqrt(L) / t[:, None]), "bv2": bf(r(L) * 0.2)}


def reference(attn1, v1, Wq2, bq2, Wk2, bk2, Wv2, bv2):
    h = np.maximum(mxq(f64(attn1), 2, "e4m3") @ mxq(f64(v1), 1, "e4m3"), 0.0)
    hq = mxq(h, 2, "e4m3")
    q2 = (hq @ mxq(f64(Wq2), 0, "e4m3")) + f64(bq2)
    k2 = (hq @ mxq(f64(Wk2), 0, "e4m3")) + f64(bk2)
    v2 = (hq @ mxq(f64(Wv2), 0, "e4m3")) + f64(bv2)
    return q2, k2, v2

@@ -1,0 +1,216 @@
+from contextlib import ExitStack
+
+import concourse.mybir as mybir
+from concourse.masks import make_identity
+
+B, S, L = 6, 512, 512
+FLOPS = B * 4 * 2 * S * S * L
+
+F32 = mybir.dt.float32
+BF16 = mybir.dt.bfloat16
+U32 = mybir.dt.uint32
+U8 = mybir.dt.uint8
+FP8X4 = mybir.dt.float8_e4m3fn_x4
+RELU = mybir.ActivationFunctionType.Relu
+ADD = mybir.AluOpType.add
+
+P = 128
+PACK = 4
+NT = 4
+H_BANK_DTYPE = F32
+
+
+def tile_perspectronencodernetwork_pa_kernel(tc, attn1, v1, Wq2, bq2, Wk2, bk2, Wv2, bv2, out_0, out_1, out_2):
+    nc = tc.nc
+    weights = (Wq2, Wk2, Wv2)
+    biases = (bq2, bk2, bv2)
+    outs = (out_0, out_1, out_2)
+
+    with ExitStack() as ctx:
+        keep = ctx.enter_context(tc.tile_pool(name="keep", bufs=1))
+        work = ctx.enter_context(tc.tile_pool(name="work", bufs=2))
+        stage = ctx.enter_context(tc.tile_pool(name="stage", bufs=6))
+        psum_t = ctx.enter_context(tc.psum_pool(name="psum_t", bufs=2))
+        psum_h = ctx.enter_context(tc.psum_pool(name="psum_h", bufs=2))
+        psum_o = ctx.enter_context(tc.psum_pool(name="psum_o", bufs=4))
+        ctx.enter_context(tc.manual_schedule())
+
+        ones = keep.tile([P, P], BF16, name="ones")
+        nc.vector.memset(ones[:], 1.0)
+        bias_rows = keep.tile([P, 3, L], BF16, name="bias_rows")
+        nc.vector.memset(bias_rows[:], 0.0)
+        ident = keep.tile([P, P], F32, name="ident")
+        make_identity(nc, ident[:])
+        warm = keep.tile([P, 1], F32, name="warm")
+        nc.scalar.activation(out=warm[:], in_=ones[:, 0:1], func=RELU)
+        bias_all = keep.tile([P, 3, L], F32, name="bias_all")
+
+        a_raw = [keep.tile([P, PACK, S], BF16, name="a_raw%d" % b) for b in range(B)]
+        v_raw = [keep.tile([P, PACK, L], BF16, name="v_raw%d" % b) for b in range(B)]
+        w_raw = [keep.tile([P, PACK, L], BF16, name="w_raw%d" % o) for o in range(3)]
+
+        def load_set(b):
+            nc.sync.dma_start(out=a_raw[b][:], in_=attn1[b].rearrange("(p j) k -> p j k", j=PACK))
+            nc.sync.dma_start(out=v_raw[b][:], in_=v1[b].rearrange("(p j) f -> p j f", j=PACK))
+
+        load_set(0)
+        for o in range(3):
+            nc.sync.dma_start(out=bias_rows[0:1, o, :], in_=biases[o].rearrange("(x n) -> x n", x=1))
+        for o in range(3):
+            nc.sync.dma_start(out=w_raw[o][:], in_=weights[o].rearrange("(p j) n -> p j n", j=PACK))
+        for b in range(1, B):
+            load_set(b)
+
+        live = {}
+
+        def transpose_attn(b):
+            words = a_raw[b][:].bitcast(F32)
+            for half in range(2):
+                xt = psum_t.tile([P, 2, 2, P], F32, tag="xt", name="xt%d_%d" % (b, half))
+                live["xt", b, half] = xt
+                for jj in range(2):
+                    for u in range(2):
+                        nc.tensor.transpose(xt[:, jj, u, :], words[:, 2 * half + jj, u : S // 2 : 2], ident[:])
+
+        def copy_attn(b):
+            ag = work.tile([P, NT, P, PACK], BF16, tag="ag", name="ag%d" % b, align_bytes=64)
+            live["ag", b] = ag
+            ag_words = ag[:].bitcast(F32)
+            for half in range(2):
+                nc.scalar.copy(
+                    out=ag_words[:, 2 * half : 2 * half + 2, :, :],
+                    in_=live["xt", b, half][:].rearrange("p j u r -> p j r u"),
+                )
+
+        def interleave_v(b, engine_copy):
+            vg = work.tile([P, PACK, P, PACK], BF16, tag="vg", name="vg%d" % b, align_bytes=64)
+            live["vg", b] = vg
+            engine_copy(out=vg[:], in_=v_raw[b][:].rearrange("p j (m t) -> p t m j", t=PACK))
+
+        def interleave_w(o, engine_copy):
+            wg = work.tile([P, L, PACK], BF16, tag="wg", name="wg%d" % o, align_bytes=64)
+            live["wg", o] = wg
+            engine_copy(out=wg[:], in_=w_raw[o][:].rearrange("p j n -> p n j"))
+
+        def quantize(kind, idx, pool, flat_in):
+            slot = kind if kind != "w" else "w%d" % idx
+            codes = pool.tile([P, S], U32, tag=slot + "_codes", name="%s_codes%d" % (kind, idx), align_bytes=64)
+            scales = pool.tile([P, S], U8, tag=slot + "_scales", name="%s_scales%d" % (kind, idx), align_bytes=64)
+            live[kind, idx] = (codes, scales)
+            nc.vector.quantize_mx(out=codes[:].bitcast(FP8X4), scales=scales[:], in_=flat_in)
+
+        def quantize_attn(b):
+            quantize("a", b, work, live["ag", b][:].rearrange("p j r t -> p (j r t)"))
+
+        def quantize_v(b):
+            quantize("v", b, work, live["vg", b][:].rearrange("p t m j -> p (t m j)"))
+
+        def quantize_w(o):
+            quantize("w", o, keep, live["wg", o][:].rearrange("p n j -> p (n j)"))
+
+        def quantize_h(b):
+            quantize("h", b, work, live["hg", b][:].rearrange("p j r t -> p (j r t)"))
+
+        def cols(i):
+            return slice(i * P, (i + 1) * P)
+
+        def stage1(b, j):
+            a_codes, a_scales = live["a", b]
+            v_codes, v_scales = live["v", b]
+            hp = psum_h.tile([P, PACK, P], H_BANK_DTYPE, tag="hp", name="hp%d_%d" % (b, j))
+            for t in range(PACK):
+                nc.tensor.matmul_mx(
+                    out=hp[:, t, :],
+                    lhsT=v_codes[:, cols(t)].bitcast(FP8X4),
+                    lhsT_scale=v_scales[:, cols(t)],
+                    rhs=a_codes[:, cols(j)].bitcast(FP8X4),
+                    rhs_scale=a_scales[:, cols(j)],
+                    start=True,
+                    stop=True,
+                )
+            if j == 0:
+                live["hg", b] = work.tile([P, NT, P, PACK], BF16, tag="hg", name="hg%d" % b, align_bytes=64)
+            nc.scalar.activation(out=live["hg", b][:, j, :, :], in_=hp[:].rearrange("p t r -> p r t"), func=RELU)
+
+        def project(b, o, j):
+            h_codes, h_scales = live["h", b]
+            w_codes, w_scales = live["w", o]
+            acc = psum_o.tile([P, L], F32, tag="acc", name="acc%d_%d_%d" % (b, o, j))
+            live["acc", b, o, j] = acc
+            nc.tensor.matmul_mx(
+                out=acc[:],
+                lhsT=h_codes[:, cols(j)].bitcast(FP8X4),
+                lhsT_scale=h_scales[:, cols(j)],
+                rhs=w_codes[:].bitcast(FP8X4),
+                rhs_scale=w_scales[:],
+                start=True,
+                stop=True,
+            )
+
+        def add_bias_and_store(b, o, j):
+            if j == 0:
+                live["st", b, o] = stage.tile([P, NT, L], F32, tag="st", name="st%d_%d" % (b, o))
+            st = live["st", b, o]
+            nc.vector.tensor_tensor(out=st[:, j, :], in0=live["acc", b, o, j][:], in1=bias_all[:, o, :], op=ADD)
+            pieces = 1 if b < B - 1 else (2 if o < 2 else 4)
+            per = NT // pieces
+            if j % per == per - 1:
+                rows = slice(j + 1 - per, j + 1)
+                nc.sync.dma_start(out=outs[o][b].rearrange("(p j) n -> p j n", j=NT)[:, rows, :], in_=st[:, rows, :])
+
+        transpose_attn(0)
+        for o in range(3):
+            bias_bank = psum_o.tile([P, L], F32, tag="acc", name="bias_bank%d" % o)
+            live["bias_bank", o] = bias_bank
+            nc.tensor.matmul(out=bias_bank[:], lhsT=ones[:], rhs=bias_rows[:, o, :], start=True, stop=True)
+        copy_attn(0)
+        interleave_v(0, nc.vector.tensor_copy)
+        quantize_attn(0)
+        quantize_v(0)
+        for o in range(3):
+            nc.scalar.copy(out=bias_all[:, o, :], in_=live["bias_bank", o][:])
+        interleave_w(0, nc.vector.tensor_copy)
+        interleave_w(1, nc.vector.tensor_copy)
+        quantize_w(0)
+        for j in range(NT):
+            stage1(0, j)
+        transpose_attn(1)
+        copy_attn(1)
+        interleave_v(1, nc.scalar.copy)
+        interleave_w(2, nc.scalar.copy)
+        quantize_h(0)
+        quantize_w(1)
+
+        banks = [(b, o, j) for b in range(B) for o in range(3) for j in range(NT)]
+        per_set = 3 * NT
+        lead = 2
+        for g in range(lead):
+            project(*banks[g])
+        for g in range(len(banks)):
+            b, o, j = banks[g]
+            s = g % per_set
+            add_bias_and_store(b, o, j)
+            if b + 1 < B and s == (3 if b == 0 else 1):
+                quantize_attn(b + 1)
+                quantize_v(b + 1)
+            if b == 0 and s == 5:
+                quantize_w(2)
+            if b + 1 < B and s == 9:
+                quantize_h(b + 1)
+            if g + lead < len(banks):
+                b2, o2, j2 = banks[g + lead]
+                s2 = (g + lead) % per_set
+                project(b2, o2, j2)
+                if b2 + 1 < B:
+                    if s2 == 5:
+                        stage1(b2 + 1, 0)
+                        stage1(b2 + 1, 1)
+                    if s2 == 6:
+                        stage1(b2 + 1, 2)
+                    if s2 == 7:
+                        stage1(b2 + 1, 3)
+                        if b2 + 2 < B:
+                            interleave_v(b2 + 2, nc.scalar.copy)
+                if b2 + 2 < B and s2 == 9:
+                    transpose_attn(b2 + 2)
+                    copy_attn(b2 + 2)

@@ -83,7 +83,7 @@ def tile_perspectronencodernetwork_pa_kernel(tc, attn1, v1, Wq2, bq2, Wk2, bk2, 
                 )
 
         def interleave_v(b, engine_copy):
-            vg = work.tile([P, PACK, P, PACK], BF16, tag="vg", name="vg%d" % b, align_bytes=64)
+            vg = work.tile([P, PACK, P, PACK], BF16, tag="vg", name="vg%d" % b, align_bytes=64, bufs=3)
             live["vg", b] = vg
             engine_copy(out=vg[:], in_=v_raw[b][:].rearrange("p j (m t) -> p t m j", t=PACK))
 
@@ -167,50 +167,62 @@ def tile_perspectronencodernetwork_pa_kernel(tc, attn1, v1, Wq2, bq2, Wk2, bk2, 
         interleave_v(0, nc.vector.tensor_copy)
         quantize_attn(0)
         quantize_v(0)
-        for o in range(3):
-            nc.scalar.copy(out=bias_all[:, o, :], in_=live["bias_bank", o][:])
-        interleave_w(0, nc.vector.tensor_copy)
+        interleave_w(0, nc.scalar.copy)
         interleave_w(1, nc.vector.tensor_copy)
         quantize_w(0)
+        interleave_w(2, nc.vector.tensor_copy)
+        quantize_w(1)
         for j in range(NT):
             stage1(0, j)
+        for o in range(3):
+            nc.scalar.copy(out=bias_all[:, o, :], in_=live["bias_bank", o][:])
         transpose_attn(1)
         copy_attn(1)
-        interleave_v(1, nc.scalar.copy)
-        interleave_w(2, nc.scalar.copy)
         quantize_h(0)
-        quantize_w(1)
+        for k in range(4):
+            project(0, k // NT, k % NT)
+        quantize_w(2)
+        transpose_attn(2)
+        interleave_v(2, nc.scalar.copy)
+        copy_attn(2)
 
-        banks = [(b, o, j) for b in range(B) for o in range(3) for j in range(NT)]
         per_set = 3 * NT
-        lead = 2
-        for g in range(lead):
-            project(*banks[g])
-        for g in range(len(banks)):
-            b, o, j = banks[g]
-            s = g % per_set
-            add_bias_and_store(b, o, j)
-            if b + 1 < B and s == (3 if b == 0 else 1):
-                quantize_attn(b + 1)
-                quantize_v(b + 1)
-            if b == 0 and s == 5:
-                quantize_w(2)
-            if b + 1 < B and s == 9:
+        for b in range(B):
+            if 0 < b < B - 1:
+                stage1(b + 1, 0)
+                stage1(b + 1, 1)
+            last = b + 2 >= B
+            k2, k3 = (1, 2) if last else (6, 7)
+            for k in range(per_set):
+                add_bias_and_store(b, k // NT, k % NT)
+                if k + 4 < per_set:
+                    project(b, (k + 4) // NT, (k + 4) % NT)
+                if b == 0 and k == 1:
+                    interleave_v(1, nc.vector.tensor_copy)
+                    quantize_attn(1)
+                    quantize_v(1)
+                    stage1(1, 0)
+                    stage1(1, 1)
+                if b + 1 < B and k == k2:
+                    stage1(b + 1, 2)
+                if b + 1 < B and k == k3:
+                    stage1(b + 1, 3)
+                if b + 3 < B and k == k3:
+                    transpose_attn(b + 3)
+                    interleave_v(b + 3, nc.scalar.copy)
+                    copy_attn(b + 3)
+                if last and b + 1 < B:
+                    if k == 9:
+                        quantize_h(b + 1)
+                        project(b + 1, 0, 0)
+                        project(b + 1, 0, 1)
+                    if k == 10:
+                        project(b + 1, 0, 2)
+                    if k == 11:
+                        project(b + 1, 0, 3)
+            if not last:
                 quantize_h(b + 1)
-            if g + lead < len(banks):
-                b2, o2, j2 = banks[g + lead]
-                s2 = (g + lead) % per_set
-                project(b2, o2, j2)
-                if b2 + 1 < B:
-                    if s2 == 5:
-                        stage1(b2 + 1, 0)
-                        stage1(b2 + 1, 1)
-                    if s2 == 6:
-                        stage1(b2 + 1, 2)
-                    if s2 == 7:
-                        stage1(b2 + 1, 3)
-                        if b2 + 2 < B:
-                            interleave_v(b2 + 2, nc.scalar.copy)
-                if b2 + 2 < B and s2 == 9:
-                    transpose_attn(b2 + 2)
-                    copy_attn(b2 + 2)
+                for j in range(NT):
+                    project(b + 1, 0, j)
+                quantize_v(b + 2)
+                quantize_attn(b + 2)

@@ -13,6 +13,7 @@ U8 = mybir.dt.uint8
 FP8X4 = mybir.dt.float8_e4m3fn_x4
 RELU = mybir.ActivationFunctionType.Relu
 ADD = mybir.AluOpType.add
+MULT = mybir.AluOpType.mult
 
 P = 128
 PACK = 4
@@ -87,10 +88,16 @@ def tile_perspectronencodernetwork_pa_kernel(tc, attn1, v1, Wq2, bq2, Wk2, bk2, 
             live["vg", b] = vg
             engine_copy(out=vg[:], in_=v_raw[b][:].rearrange("p j (m t) -> p t m j", t=PACK))
 
+        def gpsimd_copy(out, in_):
+            nc.gpsimd.tensor_scalar(out=out, in0=in_, scalar1=1.0, scalar2=0.0, op0=MULT, op1=ADD)
+
         def interleave_w(o, engine_copy):
             wg = work.tile([P, L, PACK], BF16, tag="wg", name="wg%d" % o, align_bytes=64)
             live["wg", o] = wg
-            engine_copy(out=wg[:], in_=w_raw[o][:].rearrange("p j n -> p n j"))
+            engine_copy(
+                out=wg[:].rearrange("p (c i) j -> p c j i", i=PACK),
+                in_=w_raw[o][:].rearrange("p j (c i) -> p c j i", i=PACK),
+            )
 
         def quantize(kind, idx, pool, flat_in):
             slot = kind if kind != "w" else "w%d" % idx
@@ -158,6 +165,9 @@ def tile_perspectronencodernetwork_pa_kernel(tc, attn1, v1, Wq2, bq2, Wk2, bk2, 
                 rows = slice(j + 1 - per, j + 1)
                 nc.sync.dma_start(out=outs[o][b].rearrange("(p j) n -> p j n", j=NT)[:, rows, :], in_=st[:, rows, :])
 
+        def copy_bias(o):
+            nc.scalar.copy(out=bias_all[:, o, :], in_=live["bias_bank", o][:])
+
         transpose_attn(0)
         for o in range(3):
             bias_bank = psum_o.tile([P, L], F32, tag="acc", name="bias_bank%d" % o)
@@ -168,20 +178,24 @@ def tile_perspectronencodernetwork_pa_kernel(tc, attn1, v1, Wq2, bq2, Wk2, bk2, 
         quantize_attn(0)
         quantize_v(0)
         interleave_w(0, nc.scalar.copy)
+        copy_bias(0)
         interleave_w(1, nc.vector.tensor_copy)
         quantize_w(0)
         interleave_w(2, nc.vector.tensor_copy)
         quantize_w(1)
         for j in range(NT):
             stage1(0, j)
-        for o in range(3):
-            nc.scalar.copy(out=bias_all[:, o, :], in_=live["bias_bank", o][:])
+        copy_bias(1)
+        copy_bias(2)
         transpose_attn(1)
         copy_attn(1)
+        quantize_w(2)
         quantize_h(0)
         for k in range(4):
             project(0, k // NT, k % NT)
-        quantize_w(2)
+        fence = keep.tile([P, 1], U32, name="fence")
+        nc.gpsimd.tensor_copy(out=fence[:], in_=live["h", 0][0][:, 0:1])
+        interleave_v(1, gpsimd_copy)
         transpose_attn(2)
         interleave_v(2, nc.scalar.copy)
         copy_attn(2)
@@ -197,10 +211,9 @@ def tile_perspectronencodernetwork_pa_kernel(tc, attn1, v1, Wq2, bq2, Wk2, bk2, 
                 add_bias_and_store(b, k // NT, k % NT)
                 if k + 4 < per_set:
                     project(b, (k + 4) // NT, (k + 4) % NT)
-                if b == 0 and k == 1:
-                    interleave_v(1, nc.vector.tensor_copy)
-                    quantize_attn(1)
+                if b == 0 and k == 4:
                     quantize_v(1)
+                    quantize_attn(1)
                     stage1(1, 0)
                     stage1(1, 1)
                 if b + 1 < B and k == k2:

from contextlib import ExitStack

import concourse.mybir as mybir
from concourse.masks import make_identity

B, S, L = 6, 512, 512
FLOPS = B * 4 * 2 * S * S * L

F32 = mybir.dt.float32
BF16 = mybir.dt.bfloat16
U32 = mybir.dt.uint32
U8 = mybir.dt.uint8
FP8X4 = mybir.dt.float8_e4m3fn_x4
RELU = mybir.ActivationFunctionType.Relu
ADD = mybir.AluOpType.add
MULT = mybir.AluOpType.mult

P = 128
PACK = 4
NT = 4
H_BANK_DTYPE = F32


def tile_perspectronencodernetwork_pa_kernel(tc, attn1, v1, Wq2, bq2, Wk2, bk2, Wv2, bv2, out_0, out_1, out_2):
    nc = tc.nc
    weights = (Wq2, Wk2, Wv2)
    biases = (bq2, bk2, bv2)
    outs = (out_0, out_1, out_2)

    with ExitStack() as ctx:
        keep = ctx.enter_context(tc.tile_pool(name="keep", bufs=1))
        work = ctx.enter_context(tc.tile_pool(name="work", bufs=2))
        stage = ctx.enter_context(tc.tile_pool(name="stage", bufs=6))
        psum_t = ctx.enter_context(tc.psum_pool(name="psum_t", bufs=2))
        psum_h = ctx.enter_context(tc.psum_pool(name="psum_h", bufs=2))
        psum_o = ctx.enter_context(tc.psum_pool(name="psum_o", bufs=4))
        ctx.enter_context(tc.manual_schedule())

        ones = keep.tile([P, P], BF16, name="ones")
        nc.vector.memset(ones[:], 1.0)
        bias_rows = keep.tile([P, 3, L], BF16, name="bias_rows")
        nc.vector.memset(bias_rows[:], 0.0)
        ident = keep.tile([P, P], F32, name="ident")
        make_identity(nc, ident[:])
        warm = keep.tile([P, 1], F32, name="warm")
        nc.scalar.activation(out=warm[:], in_=ones[:, 0:1], func=RELU)
        bias_all = keep.tile([P, 3, L], F32, name="bias_all")

        a_raw = [keep.tile([P, PACK, S], BF16, name="a_raw%d" % b) for b in range(B)]
        v_raw = [keep.tile([P, PACK, L], BF16, name="v_raw%d" % b) for b in range(B)]
        w_raw = [keep.tile([P, PACK, L], BF16, name="w_raw%d" % o) for o in range(3)]

        def load_set(b):
            nc.sync.dma_start(out=a_raw[b][:], in_=attn1[b].rearrange("(p j) k -> p j k", j=PACK))
            nc.sync.dma_start(out=v_raw[b][:], in_=v1[b].rearrange("(p j) f -> p j f", j=PACK))

        load_set(0)
        for o in range(3):
            nc.sync.dma_start(out=bias_rows[0:1, o, :], in_=biases[o].rearrange("(x n) -> x n", x=1))
        for o in range(3):
            nc.sync.dma_start(out=w_raw[o][:], in_=weights[o].rearrange("(p j) n -> p j n", j=PACK))
        for b in range(1, B):
            load_set(b)

        live = {}

        def transpose_attn(b):
            words = a_raw[b][:].bitcast(F32)
            for half in range(2):
                xt = psum_t.tile([P, 2, 2, P], F32, tag="xt", name="xt%d_%d" % (b, half))
                live["xt", b, half] = xt
                for jj in range(2):
                    for u in range(2):
                        nc.tensor.transpose(xt[:, jj, u, :], words[:, 2 * half + jj, u : S // 2 : 2], ident[:])

        def copy_attn(b):
            ag = work.tile([P, NT, P, PACK], BF16, tag="ag", name="ag%d" % b, align_bytes=64)
            live["ag", b] = ag
            ag_words = ag[:].bitcast(F32)
            for half in range(2):
                nc.scalar.copy(
                    out=ag_words[:, 2 * half : 2 * half + 2, :, :],
                    in_=live["xt", b, half][:].rearrange("p j u r -> p j r u"),
                )

        def interleave_v(b, engine_copy):
            vg = work.tile([P, PACK, P, PACK], BF16, tag="vg", name="vg%d" % b, align_bytes=64, bufs=3)
            live["vg", b] = vg
            engine_copy(out=vg[:], in_=v_raw[b][:].rearrange("p j (m t) -> p t m j", t=PACK))

        def gpsimd_copy(out, in_):
            nc.gpsimd.tensor_scalar(out=out, in0=in_, scalar1=1.0, scalar2=0.0, op0=MULT, op1=ADD)

        def interleave_w(o, engine_copy):
            wg = work.tile([P, L, PACK], BF16, tag="wg", name="wg%d" % o, align_bytes=64)
            live["wg", o] = wg
            engine_copy(
                out=wg[:].rearrange("p (c i) j -> p c j i", i=PACK),
                in_=w_raw[o][:].rearrange("p j (c i) -> p c j i", i=PACK),
            )

        def quantize(kind, idx, pool, flat_in):
            slot = kind if kind != "w" else "w%d" % idx
            codes = pool.tile([P, S], U32, tag=slot + "_codes", name="%s_codes%d" % (kind, idx), align_bytes=64)
            scales = pool.tile([P, S], U8, tag=slot + "_scales", name="%s_scales%d" % (kind, idx), align_bytes=64)
            live[kind, idx] = (codes, scales)
            nc.vector.quantize_mx(out=codes[:].bitcast(FP8X4), scales=scales[:], in_=flat_in)

        def quantize_attn(b):
            quantize("a", b, work, live["ag", b][:].rearrange("p j r t -> p (j r t)"))

        def quantize_v(b):
            quantize("v", b, work, live["vg", b][:].rearrange("p t m j -> p (t m j)"))

        def quantize_w(o):
            quantize("w", o, keep, live["wg", o][:].rearrange("p n j -> p (n j)"))

        def quantize_h(b):
            quantize("h", b, work, live["hg", b][:].rearrange("p j r t -> p (j r t)"))

        def cols(i):
            return slice(i * P, (i + 1) * P)

        def stage1(b, j):
            a_codes, a_scales = live["a", b]
            v_codes, v_scales = live["v", b]
            hp = psum_h.tile([P, PACK, P], H_BANK_DTYPE, tag="hp", name="hp%d_%d" % (b, j))
            for t in range(PACK):
                nc.tensor.matmul_mx(
                    out=hp[:, t, :],
                    lhsT=v_codes[:, cols(t)].bitcast(FP8X4),
                    lhsT_scale=v_scales[:, cols(t)],
                    rhs=a_codes[:, cols(j)].bitcast(FP8X4),
                    rhs_scale=a_scales[:, cols(j)],
                    start=True,
                    stop=True,
                )
            if j == 0:
                live["hg", b] = work.tile([P, NT, P, PACK], BF16, tag="hg", name="hg%d" % b, align_bytes=64)
            nc.scalar.activation(out=live["hg", b][:, j, :, :], in_=hp[:].rearrange("p t r -> p r t"), func=RELU)

        def project(b, o, j):
            h_codes, h_scales = live["h", b]
            w_codes, w_scales = live["w", o]
            acc = psum_o.tile([P, L], F32, tag="acc", name="acc%d_%d_%d" % (b, o, j))
            live["acc", b, o, j] = acc
            nc.tensor.matmul_mx(
                out=acc[:],
                lhsT=h_codes[:, cols(j)].bitcast(FP8X4),
                lhsT_scale=h_scales[:, cols(j)],
                rhs=w_codes[:].bitcast(FP8X4),
                rhs_scale=w_scales[:],
                start=True,
                stop=True,
            )

        def add_bias_and_store(b, o, j):
            if j == 0:
                live["st", b, o] = stage.tile([P, NT, L], F32, tag="st", name="st%d_%d" % (b, o))
            st = live["st", b, o]
            nc.vector.tensor_tensor(out=st[:, j, :], in0=live["acc", b, o, j][:], in1=bias_all[:, o, :], op=ADD)
            pieces = 1 if b < B - 1 else (2 if o < 2 else 4)
            per = NT // pieces
            if j % per == per - 1:
                rows = slice(j + 1 - per, j + 1)
                nc.sync.dma_start(out=outs[o][b].rearrange("(p j) n -> p j n", j=NT)[:, rows, :], in_=st[:, rows, :])

        def copy_bias(o):
            nc.scalar.copy(out=bias_all[:, o, :], in_=live["bias_bank", o][:])

        transpose_attn(0)
        for o in range(3):
            bias_bank = psum_o.tile([P, L], F32, tag="acc", name="bias_bank%d" % o)
            live["bias_bank", o] = bias_bank
            nc.tensor.matmul(out=bias_bank[:], lhsT=ones[:], rhs=bias_rows[:, o, :], start=True, stop=True)
        copy_attn(0)
        interleave_v(0, nc.vector.tensor_copy)
        quantize_attn(0)
        quantize_v(0)
        interleave_w(0, nc.scalar.copy)
        copy_bias(0)
        interleave_w(1, nc.vector.tensor_copy)
        quantize_w(0)
        interleave_w(2, nc.vector.tensor_copy)
        quantize_w(1)
        for j in range(NT):
            stage1(0, j)
        copy_bias(1)
        copy_bias(2)
        transpose_attn(1)
        copy_attn(1)
        quantize_w(2)
        quantize_h(0)
        for k in range(4):
            project(0, k // NT, k % NT)
        fence = keep.tile([P, 1], U32, name="fence")
        nc.gpsimd.tensor_copy(out=fence[:], in_=live["h", 0][0][:, 0:1])
        interleave_v(1, gpsimd_copy)
        transpose_attn(2)
        interleave_v(2, nc.scalar.copy)
        copy_attn(2)

        per_set = 3 * NT
        for b in range(B):
            if 0 < b < B - 1:
                stage1(b + 1, 0)
                stage1(b + 1, 1)
            last = b + 2 >= B
            k2, k3 = (1, 2) if last else (6, 7)
            for k in range(per_set):
                add_bias_and_store(b, k // NT, k % NT)
                if k + 4 < per_set:
                    project(b, (k + 4) // NT, (k + 4) % NT)
                if b == 0 and k == 4:
                    quantize_v(1)
                    quantize_attn(1)
                    stage1(1, 0)
                    stage1(1, 1)
                if b + 1 < B and k == k2:
                    stage1(b + 1, 2)
                if b + 1 < B and k == k3:
                    stage1(b + 1, 3)
                if b + 3 < B and k == k3:
                    transpose_attn(b + 3)
                    interleave_v(b + 3, nc.scalar.copy)
                    copy_attn(b + 3)
                if last and b + 1 < B:
                    if k == 9:
                        quantize_h(b + 1)
                        project(b + 1, 0, 0)
                        project(b + 1, 0, 1)
                    if k == 10:
                        project(b + 1, 0, 2)
                    if k == 11:
                        project(b + 1, 0, 3)
            if not last:
                quantize_h(b + 1)
                for j in range(NT):
                    project(b + 1, 0, j)
                quantize_v(b + 2)
                quantize_attn(b + 2)
